import numpy as np
import ml_dtypes


def mxq(x, axis, fmt="e4m3"):
    dtype, down = {"e4m3": (ml_dtypes.float8_e4m3fn, 7), "e5m2": (ml_dtypes.float8_e5m2, 14)}[fmt]
    v = np.moveaxis(np.asarray(x, np.float32).astype(ml_dtypes.bfloat16).astype(np.float64), axis, -1)
    blocks = v.reshape(v.shape[:-1] + (-1, 32))
    amax = np.abs(blocks).max(-1, keepdims=True)
    byte = np.maximum(np.where(amax > 0, np.frexp(amax)[1] - 1 + 127, 0) - down, 1)
    scale = np.exp2(byte - 127.0)
    codes = (blocks / scale).astype(np.float32).astype(dtype).astype(np.float64)
    return np.moveaxis((codes * scale).reshape(v.shape), -1, axis)


WIDE = False


def mx_kscale(k):
    if not WIDE:
        return np.ones(k)
    levels = np.array([10, -10, 5, -5, 0])
    a = np.random.permutation(np.resize(levels, k // 512 * 4)).reshape(k // 512, 4)
    idx = np.arange(k)
    return np.exp2(a[idx // 512, idx % 128 // 32])


BF16 = ml_dtypes.bfloat16


def bf(x):
    return np.asarray(x, np.float32).astype(BF16)


def f64(x):
    return np.asarray(x).astype(np.float64)


E2M1 = np.array([0.0, 0.5, 1.0, 1.5, 2.0, 3.0, 4.0, 6.0, -0.0, -0.5, -1.0, -1.5, -2.0, -3.0, -4.0, -6.0])


def pack_weight(w, fmt):
    k, n = w.shape
    w = f64(bf(w)).reshape(k // 32, 32, n)
    amax = np.abs(w).max(1)
    if fmt == "e4m3":
        byte = np.frexp(amax)[1] - 1 + 127 - 7
    else:
        mant, ex = np.frexp(amax / 6.0)
        byte = np.where(mant > 0.5, ex, ex - 1) + 127
    byte = np.clip(np.where(amax > 0, byte, 1), 1, 254)
    scaled = (w * np.exp2(127.0 - byte)[:, None, :]).reshape(k, n).astype(np.float32)
    by_word = np.ascontiguousarray(scaled.reshape(k // 512, 128, 4, n).transpose(0, 1, 3, 2))
    if fmt == "e4m3":
        words = by_word.astype(ml_dtypes.float8_e4m3fn).view(np.uint8)
    else:
        c = by_word.astype(ml_dtypes.float4_e2m1fn).view(np.uint8) & 0xF
        words = c[..., 0::2] | (c[..., 1::2] << 4)
    return np.ascontiguousarray(words), np.ascontiguousarray(byte.astype(np.uint8).reshape(k // 512, 16, n))


def unpack_weight(words, scales, fmt):
    g, p, n, _ = words.shape
    if fmt == "e4m3":
        vals = np.ascontiguousarray(words).view(ml_dtypes.float8_e4m3fn).astype(np.float64)
    else:
        nib = np.empty((g, p, n, 4), np.uint8)
        nib[..., 0::2] = words & 0xF
        nib[..., 1::2] = words >> 4
        vals = E2M1[nib]
    vals = vals * np.repeat(np.exp2(scales.astype(np.float64) - 127.0), 8, axis=1)[..., None]
    return vals.transpose(0, 1, 3, 2).reshape(g * 512, n)


B, N, DIM, HEADS, MID = 1, 128, 512, 8, 8192
FMT = "e4m3"


def conprefix(xq, dw, db, uw, ub):
    h = np.tanh((xq @ dw) + f64(db))
    kv = (mxq(h, 2, "e4m3") @ uw) + f64(ub)
    return np.concatenate([np.zeros((B, N, DIM)), kv], axis=-1)


def setup_inputs():
    s = mx_kscale(DIM)
    a, m = 1.0 / np.sqrt(DIM), 1.0 / np.sqrt(MID)
    x = bf(np.random.standard_normal((B, N, DIM)) * s)
    Wqkv_words, Wqkv_scales = pack_weight((np.random.standard_normal((3 * DIM, DIM)) * a / s).T, FMT)
    down_w_words, down_w_scales = pack_weight((np.random.standard_normal((MID, DIM)) * a / s).T, FMT)
    down_b = bf(np.random.standard_normal(MID) * 0.3)
    up_w_words, up_w_scales = pack_weight((np.random.standard_normal((2 * DIM, MID)) * m).T, FMT)
    up_b = bf(np.random.standard_normal(2 * DIM) * 0.3)
    pdown_w_words, pdown_w_scales = pack_weight((np.random.standard_normal((MID, DIM)) * a / s).T, FMT)
    pdown_b = bf(np.random.standard_normal(MID) * 0.3)
    pup_w_words, pup_w_scales = pack_weight((np.random.standard_normal((2 * DIM, MID)) * m).T, FMT)
    pup_b = bf(np.random.standard_normal(2 * DIM) * 0.3)
    return {
        "x": x,
        "Wqkv_words": Wqkv_words,
        "Wqkv_scales": Wqkv_scales,
        "down_w_words": down_w_words,
        "down_w_scales": down_w_scales,
        "down_b": down_b,
        "up_w_words": up_w_words,
        "up_w_scales": up_w_scales,
        "up_b": up_b,
        "pdown_w_words": pdown_w_words,
        "pdown_w_scales": pdown_w_scales,
        "pdown_b": pdown_b,
        "pup_w_words": pup_w_words,
        "pup_w_scales": pup_w_scales,
        "pup_b": pup_b,
    }


def reference(x, Wqkv_words, Wqkv_scales, down_w_words, down_w_scales, down_b, up_w_words, up_w_scales, up_b,
              pdown_w_words, pdown_w_scales, pdown_b, pup_w_words, pup_w_scales, pup_b):
    xq = mxq(f64(x), 2, "e4m3")
    qkv = xq @ unpack_weight(Wqkv_words, Wqkv_scales, FMT)
    return (qkv + conprefix(xq, unpack_weight(pdown_w_words, pdown_w_scales, FMT), pdown_b,
                            unpack_weight(pup_w_words, pup_w_scales, FMT), pup_b)
                + conprefix(xq, unpack_weight(down_w_words, down_w_scales, FMT), down_b,
                            unpack_weight(up_w_words, up_w_scales, FMT), up_b))

@@ -1,0 +1,301 @@
+from contextlib import ExitStack
+
+import concourse.mybir as mybir
+from concourse.masks import make_identity
+
+F32 = mybir.dt.float32
+BF16 = mybir.dt.bfloat16
+I32 = mybir.dt.int32
+U32 = mybir.dt.uint32
+U8 = mybir.dt.uint8
+FP8X4 = mybir.dt.float8_e4m3fn_x4
+TANH = mybir.ActivationFunctionType.Tanh
+ADD = mybir.AluOpType.add
+
+P = 128
+PACK = 4
+K_PASS = P * PACK
+BANK = 512
+DIM = 512
+HIDDEN = 8192
+KV = 1024
+ADAPTERS = 2
+QUADRANTS = 4
+
+GROUPS = ADAPTERS * HIDDEN // K_PASS
+ROUND = 4
+ROUNDS = GROUPS // ROUND
+UP_PIECE = 2
+UP_PIECES = GROUPS // UP_PIECE
+PIECE_BUFS = 16
+UP_LAG = 22
+
+FLOPS = 2 * P * (DIM * (DIM + KV) + ADAPTERS * (DIM * HIDDEN + HIDDEN * KV))
+
+
+def tile_attention_pa_k_kernel(
+    tc,
+    x,
+    Wqkv_words,
+    Wqkv_scales,
+    down_w_words,
+    down_w_scales,
+    down_b,
+    up_w_words,
+    up_w_scales,
+    up_b,
+    pdown_w_words,
+    pdown_w_scales,
+    pdown_b,
+    pup_w_words,
+    pup_w_scales,
+    pup_b,
+    out,
+):
+    nc = tc.nc
+    down_words = [pdown_w_words, down_w_words]
+    down_scales = [pdown_w_scales, down_w_scales]
+    down_bias = [pdown_b, down_b]
+    up_words = [pup_w_words, up_w_words]
+    up_scales = [pup_w_scales, up_w_scales]
+    up_bias = [pup_b, up_b]
+
+    with ExitStack() as pools:
+        keep = pools.enter_context(tc.tile_pool(name="keep", bufs=1))
+        pieces = pools.enter_context(tc.tile_pool(name="pieces", bufs=PIECE_BUFS))
+        sorted_pool = pools.enter_context(tc.tile_pool(name="sorted", bufs=4))
+        hidden_pool = pools.enter_context(tc.tile_pool(name="hidden", bufs=2))
+        sums = pools.enter_context(tc.psum_pool(name="sums", bufs=1))
+        banks = pools.enter_context(tc.psum_pool(name="banks", bufs=3))
+
+        round_cols = ROUND * BANK
+        first_planes = keep.tile([P, BANK + ADAPTERS * round_cols], U8, align_bytes=64)
+        up_planes = keep.tile([P, ROUNDS * KV], U8, align_bytes=64)
+        nc.vector.memset(first_planes[:].bitcast(I32), 0)
+        nc.vector.memset(up_planes[:].bitcast(I32), 0)
+
+        identity = keep.tile([P, P], F32)
+        make_identity(nc, identity[:])
+        ones = keep.tile([P, P], BF16)
+        nc.gpsimd.memset(ones[:], 1.0)
+        down_bias_rows = keep.tile([P, K_PASS], BF16)
+        nc.gpsimd.memset(down_bias_rows[:], 0.0)
+        up_bias_rows = keep.tile([P, KV], BF16)
+        nc.gpsimd.memset(up_bias_rows[:], 0.0)
+        spare = keep.tile([P, 1], F32)
+        nc.vector.memset(spare[:], 0.0)
+        nc.scalar.activation(out=spare[:], in_=spare[:], func=TANH)
+
+        x_rows = keep.tile([P, DIM], BF16)
+        nc.scalar.dma_start(out=x_rows[:], in_=x[0])
+        for a in range(ADAPTERS):
+            first = a * GROUPS // ADAPTERS
+            nc.scalar.dma_start(
+                out=down_bias_rows[first : first + GROUPS // ADAPTERS, :],
+                in_=down_bias[a].rearrange("(g c) -> g c", c=K_PASS),
+            )
+            nc.scalar.dma_start(out=up_bias_rows[a : a + 1, :], in_=up_bias[a].rearrange("(o n) -> o n", o=1))
+
+        qkv_words = keep.tile([P, DIM + KV], I32, align_bytes=64)
+        nc.sync.dma_start(out=qkv_words[:], in_=Wqkv_words[0].rearrange("p n t -> p (n t)").bitcast(I32))
+
+        def load_planes(planes, cols, count, rows_of):
+            for quadrant in range(QUADRANTS):
+                nc.sync.dma_start(
+                    out=planes[32 * quadrant : 32 * quadrant + 4 * count, cols].bitcast(I32),
+                    in_=rows_of(slice(4 * quadrant, 4 * quadrant + 4)).bitcast(I32),
+                )
+
+        load_planes(
+            first_planes,
+            slice(0, BANK),
+            3,
+            lambda rows: Wqkv_scales[0][rows, :].rearrange("r (j n) -> j r n", n=BANK),
+        )
+        for a in range(ADAPTERS):
+            load_planes(
+                first_planes,
+                slice(BANK + a * round_cols, BANK + (a + 1) * round_cols),
+                ROUND,
+                lambda rows: down_scales[a][0][rows, :].rearrange("r (j n) -> j r n", n=round_cols),
+            )
+
+        down_piece = []
+        for r in range(ROUNDS):
+            a = r // (ROUNDS // ADAPTERS)
+            first = (r % (ROUNDS // ADAPTERS)) * round_cols * PACK
+            piece = pieces.tile([P, round_cols], I32, tag="piece", align_bytes=64)
+            nc.sync.dma_start(
+                out=piece[:],
+                in_=down_words[a][0].rearrange("p n t -> p (n t)")[:, first : first + round_cols * PACK].bitcast(I32),
+            )
+            down_piece.append(piece)
+
+        for r in range(ROUNDS):
+            a = r // (ROUNDS // ADAPTERS)
+            first = (r % (ROUNDS // ADAPTERS)) * ROUND
+            load_planes(
+                up_planes,
+                slice(r * KV, (r + 1) * KV),
+                ROUND,
+                lambda rows: up_scales[a][first : first + ROUND, rows, :],
+            )
+
+        up_piece = []
+
+        def load_up_piece():
+            u = len(up_piece)
+            a = u // (UP_PIECES // ADAPTERS)
+            first = (u % (UP_PIECES // ADAPTERS)) * UP_PIECE
+            piece = pieces.tile([P, UP_PIECE, KV], I32, tag="piece", align_bytes=64)
+            nc.sync.dma_start(
+                out=piece[:],
+                in_=up_words[a][first : first + UP_PIECE].rearrange("g p n t -> p g (n t)").bitcast(I32),
+            )
+            up_piece.append(piece)
+
+        for u in range(PIECE_BUFS - ROUNDS):
+            load_up_piece()
+
+        x_words = x_rows[:].bitcast(F32)
+        x_turned = banks.tile([P, 2, P], F32, tag="turned")
+        for u in range(2):
+            nc.tensor.transpose(x_turned[:, u, :], x_words[:, u : DIM // 2 : 2], identity[:])
+        x_grouped = keep.tile([P, K_PASS], BF16, align_bytes=64)
+        nc.vector.tensor_copy(
+            out=x_grouped[:].bitcast(F32).rearrange("p (w u) -> p w u", u=2),
+            in_=x_turned[:].rearrange("p u w -> p w u"),
+        )
+        x_codes = keep.tile([P, P], U32, align_bytes=64)
+        x_scales = keep.tile([P, P], U8, align_bytes=64)
+        nc.vector.quantize_mx(out=x_codes[:].bitcast(FP8X4), scales=x_scales[:], in_=x_grouped[:])
+
+        down_bias_sorted = keep.tile([P, PACK, P], F32)
+        nc.vector.tensor_copy(out=down_bias_sorted[:], in_=down_bias_rows[:].rearrange("g (p t) -> g t p", t=PACK))
+        bias_turned = banks.tile([P, PACK, P], F32, tag="turned")
+        for t in range(PACK):
+            nc.tensor.transpose(bias_turned[:, t, :], down_bias_sorted[:, t, :], identity[:])
+        down_bias_cols = keep.tile([P, PACK, GROUPS], F32)
+        nc.vector.tensor_copy(out=down_bias_cols[:], in_=bias_turned[:, :, 0:GROUPS])
+
+        kv_bias = keep.tile([P, KV], F32)
+        for half in range(KV // BANK):
+            cols = slice(half * BANK, (half + 1) * BANK)
+            spread = banks.tile([P, BANK], F32, tag="product")
+            nc.tensor.matmul(out=spread[:], lhsT=ones[:], rhs=up_bias_rows[:, cols], start=True, stop=True)
+            nc.scalar.copy(out=kv_bias[:, cols], in_=spread[:])
+
+        def multiply_x(bank, words, planes, start, stop):
+            nc.tensor.matmul_mx(
+                out=bank,
+                lhsT=x_codes[:].bitcast(FP8X4),
+                lhsT_scale=x_scales[:],
+                rhs=words.bitcast(FP8X4),
+                rhs_scale=planes,
+                start=start,
+                stop=stop,
+            )
+
+        query_bank = banks.tile([P, BANK], F32, tag="product")
+        multiply_x(query_bank[:], qkv_words[:, 0:BANK], first_planes[0:P, 0:BANK], True, True)
+        query = keep.tile([P, BANK], F32)
+        nc.scalar.copy(out=query[:], in_=query_bank[:])
+        nc.scalar.dma_start(out=out[0][:, 0:BANK], in_=query[:])
+
+        kv_sum = [sums.tile([P, BANK], F32, name="kv_sum%d" % half) for half in range(KV // BANK)]
+        for half in range(KV // BANK):
+            block = 1 + half
+            multiply_x(
+                kv_sum[half][:],
+                qkv_words[:, block * BANK : (block + 1) * BANK],
+                first_planes[4 * block : P, 0:BANK],
+                True,
+                False,
+            )
+
+        h_codes = keep.tile([P, GROUPS * P], U32, align_bytes=64)
+        h_scales = keep.tile([P, GROUPS * P], U8, align_bytes=64)
+        sorted_rows = {}
+        h_planes = {}
+        h_grouped = {}
+
+        def multiply_down(group):
+            r, c = divmod(group, ROUND)
+            a, j = divmod(r, ROUNDS // ADAPTERS)
+            first = BANK + a * round_cols + c * BANK
+            product = banks.tile([P, BANK], F32, tag="product")
+            multiply_x(
+                product[:],
+                down_piece[r][:, c * BANK : (c + 1) * BANK],
+                first_planes[4 * j : P, first : first + BANK],
+                True,
+                True,
+            )
+            by_t = sorted_pool.tile([P, PACK, P], F32, tag="by_t")
+            nc.vector.tensor_copy(out=by_t[:], in_=product[:].rearrange("w (p t) -> w t p", t=PACK))
+            sorted_rows[group] = by_t
+
+        def turn_and_squash(group):
+            r, c = divmod(group, ROUND)
+            if c == 0:
+                planes = hidden_pool.tile([P, ROUND, PACK, P], BF16, tag="planes")
+                h_planes[r] = planes
+            turned = banks.tile([P, PACK, P], F32, tag="turned")
+            for t in range(PACK):
+                nc.tensor.transpose(turned[:, t, :], sorted_rows[group][:, t, :], identity[:])
+            for t in range(PACK):
+                nc.scalar.activation(
+                    out=h_planes[r][:, c, t, :],
+                    in_=turned[:, t, :],
+                    func=TANH,
+                    bias=down_bias_cols[:, t, group : group + 1],
+                )
+
+        def regroup(r):
+            grouped = hidden_pool.tile([P, ROUND, P, PACK], BF16, tag="grouped", align_bytes=64)
+            nc.vector.tensor_copy(out=grouped[:], in_=h_planes[r][:].rearrange("p g t w -> p g w t"))
+            h_grouped[r] = grouped
+
+        def quantise(r):
+            cols = slice(r * ROUND * P, (r + 1) * ROUND * P)
+            nc.vector.quantize_mx(
+                out=h_codes[:, cols].bitcast(FP8X4),
+                scales=h_scales[:, cols],
+                in_=h_grouped[r][:].rearrange("p g w t -> p (g w t)"),
+            )
+
+        def multiply_up(group):
+            u, i = divmod(group, UP_PIECE)
+            r, j = divmod(group, ROUND)
+            tokens = slice(group * P, (group + 1) * P)
+            for half in range(KV // BANK):
+                cols = slice(half * BANK, (half + 1) * BANK)
+                nc.tensor.matmul_mx(
+                    out=kv_sum[half][:],
+                    lhsT=h_codes[:, tokens].bitcast(FP8X4),
+                    lhsT_scale=h_scales[:, tokens],
+                    rhs=up_piece[u][:, i, cols].bitcast(FP8X4),
+                    rhs_scale=up_planes[4 * j : P, r * KV + half * BANK : r * KV + (half + 1) * BANK],
+                    start=False,
+                    stop=(group == GROUPS - 1),
+                )
+
+        for step in range(GROUPS + UP_LAG):
+            if step < GROUPS:
+                multiply_down(step)
+                if step % ROUND == ROUND - 1:
+                    load_up_piece()
+            if 0 <= step - 1 < GROUPS:
+                turn_and_squash(step - 1)
+                if (step - 1) % ROUND == ROUND - 1:
+                    regroup((step - 1) // ROUND)
+            if 0 <= step - 2 < GROUPS and (step - 2) % ROUND == ROUND - 1:
+                quantise((step - 2) // ROUND)
+            if step >= UP_LAG:
+                multiply_up(step - UP_LAG)
+
+        kv_out = keep.tile([P, KV], F32)
+        for half in range(KV // BANK):
+            cols = slice(half * BANK, (half + 1) * BANK)
+            nc.vector.tensor_tensor(out=kv_out[:, cols], in0=kv_sum[half][:], in1=kv_bias[:, cols], op=ADD)
+            nc.sync.dma_start(out=out[0][:, BANK + half * BANK : BANK + (half + 1) * BANK], in_=kv_out[:, cols])

@@ -29,6 +29,7 @@ UP_PIECE = 2
 UP_PIECES = GROUPS // UP_PIECE
 PIECE_BUFS = 16
 UP_LAG = 22
+RIDERS = 2
 
 FLOPS = 2 * P * (DIM * (DIM + KV) + ADAPTERS * (DIM * HIDDEN + HIDDEN * KV))
 
@@ -90,56 +91,72 @@ def tile_attention_pa_k_kernel(
         nc.scalar.dma_start(out=x_rows[:], in_=x[0])
         for a in range(ADAPTERS):
             first = a * GROUPS // ADAPTERS
-            nc.scalar.dma_start(
+            nc.gpsimd.dma_start(
                 out=down_bias_rows[first : first + GROUPS // ADAPTERS, :],
                 in_=down_bias[a].rearrange("(g c) -> g c", c=K_PASS),
             )
-            nc.scalar.dma_start(out=up_bias_rows[a : a + 1, :], in_=up_bias[a].rearrange("(o n) -> o n", o=1))
-
-        qkv_words = keep.tile([P, DIM + KV], I32, align_bytes=64)
-        nc.sync.dma_start(out=qkv_words[:], in_=Wqkv_words[0].rearrange("p n t -> p (n t)").bitcast(I32))
-
-        def load_planes(planes, cols, count, rows_of):
-            for quadrant in range(QUADRANTS):
-                nc.sync.dma_start(
-                    out=planes[32 * quadrant : 32 * quadrant + 4 * count, cols].bitcast(I32),
-                    in_=rows_of(slice(4 * quadrant, 4 * quadrant + 4)).bitcast(I32),
-                )
-
-        load_planes(
-            first_planes,
-            slice(0, BANK),
-            3,
-            lambda rows: Wqkv_scales[0][rows, :].rearrange("r (j n) -> j r n", n=BANK),
-        )
         for a in range(ADAPTERS):
-            load_planes(
+            nc.gpsimd.dma_start(out=up_bias_rows[a : a + 1, :], in_=up_bias[a].rearrange("(o n) -> o n", o=1))
+
+        def plane_dmas(planes, cols, count, rows_of):
+            return [
+                (
+                    planes[32 * quadrant : 32 * quadrant + 4 * count, cols].bitcast(I32),
+                    rows_of(slice(4 * quadrant, 4 * quadrant + 4)).bitcast(I32),
+                )
+                for quadrant in range(QUADRANTS)
+            ]
+
+        def down_plane_dmas(a):
+            return plane_dmas(
                 first_planes,
                 slice(BANK + a * round_cols, BANK + (a + 1) * round_cols),
                 ROUND,
                 lambda rows: down_scales[a][0][rows, :].rearrange("r (j n) -> j r n", n=round_cols),
             )
 
-        down_piece = []
-        for r in range(ROUNDS):
-            a = r // (ROUNDS // ADAPTERS)
-            first = (r % (ROUNDS // ADAPTERS)) * round_cols * PACK
-            piece = pieces.tile([P, round_cols], I32, tag="piece", align_bytes=64)
-            nc.sync.dma_start(
-                out=piece[:],
-                in_=down_words[a][0].rearrange("p n t -> p (n t)")[:, first : first + round_cols * PACK].bitcast(I32),
-            )
-            down_piece.append(piece)
-
-        for r in range(ROUNDS):
+        def up_plane_dmas(r):
             a = r // (ROUNDS // ADAPTERS)
             first = (r % (ROUNDS // ADAPTERS)) * ROUND
-            load_planes(
+            return plane_dmas(
                 up_planes,
                 slice(r * KV, (r + 1) * KV),
                 ROUND,
                 lambda rows: up_scales[a][first : first + ROUND, rows, :],
             )
+
+        for destination, source in down_plane_dmas(0):
+            nc.sync.dma_start(out=destination, in_=source)
+        riders = down_plane_dmas(1) + plane_dmas(
+            first_planes,
+            slice(0, BANK),
+            3,
+            lambda rows: Wqkv_scales[0][rows, :].rearrange("r (j n) -> j r n", n=BANK),
+        )
+        for r in range(ROUNDS):
+            riders.extend(up_plane_dmas(r))
+        words_loaded = []
+
+        def load_words(destination, source):
+            nc.sync.dma_start(out=destination, in_=source)
+            n = len(words_loaded)
+            for rider_destination, rider_source in riders[RIDERS * n : RIDERS * (n + 1)]:
+                nc.sync.dma_start(out=rider_destination, in_=rider_source)
+            words_loaded.append(destination)
+
+        down_piece = []
+        for r in range(ROUNDS):
+            a = r // (ROUNDS // ADAPTERS)
+            first = (r % (ROUNDS // ADAPTERS)) * round_cols * PACK
+            piece = pieces.tile([P, round_cols], I32, tag="piece", align_bytes=64)
+            load_words(
+                piece[:],
+                down_words[a][0].rearrange("p n t -> p (n t)")[:, first : first + round_cols * PACK].bitcast(I32),
+            )
+            down_piece.append(piece)
+
+        qkv_words = keep.tile([P, DIM + KV], I32, align_bytes=64)
+        load_words(qkv_words[:], Wqkv_words[0].rearrange("p n t -> p (n t)").bitcast(I32))
 
         up_piece = []
 
@@ -148,9 +165,9 @@ def tile_attention_pa_k_kernel(
             a = u // (UP_PIECES // ADAPTERS)
             first = (u % (UP_PIECES // ADAPTERS)) * UP_PIECE
             piece = pieces.tile([P, UP_PIECE, KV], I32, tag="piece", align_bytes=64)
-            nc.sync.dma_start(
-                out=piece[:],
-                in_=up_words[a][first : first + UP_PIECE].rearrange("g p n t -> p g (n t)").bitcast(I32),
+            load_words(
+                piece[:],
+                up_words[a][first : first + UP_PIECE].rearrange("g p n t -> p g (n t)").bitcast(I32),
             )
             up_piece.append(piece)
 
@@ -194,23 +211,6 @@ def tile_attention_pa_k_kernel(
                 rhs_scale=planes,
                 start=start,
                 stop=stop,
-            )
-
-        query_bank = banks.tile([P, BANK], F32, tag="product")
-        multiply_x(query_bank[:], qkv_words[:, 0:BANK], first_planes[0:P, 0:BANK], True, True)
-        query = keep.tile([P, BANK], F32)
-        nc.scalar.copy(out=query[:], in_=query_bank[:])
-        nc.scalar.dma_start(out=out[0][:, 0:BANK], in_=query[:])
-
-        kv_sum = [sums.tile([P, BANK], F32, name="kv_sum%d" % half) for half in range(KV // BANK)]
-        for half in range(KV // BANK):
-            block = 1 + half
-            multiply_x(
-                kv_sum[half][:],
-                qkv_words[:, block * BANK : (block + 1) * BANK],
-                first_planes[4 * block : P, 0:BANK],
-                True,
-                False,
             )
 
         h_codes = keep.tile([P, GROUPS * P], U32, align_bytes=64)
@@ -264,23 +264,23 @@ def tile_attention_pa_k_kernel(
                 in_=h_grouped[r][:].rearrange("p g w t -> p (g w t)"),
             )
 
-        def multiply_up(group):
-            u, i = divmod(group, UP_PIECE)
-            r, j = divmod(group, ROUND)
-            tokens = slice(group * P, (group + 1) * P)
+        def multiply_up(u):
             for half in range(KV // BANK):
-                cols = slice(half * BANK, (half + 1) * BANK)
-                nc.tensor.matmul_mx(
-                    out=kv_sum[half][:],
-                    lhsT=h_codes[:, tokens].bitcast(FP8X4),
-                    lhsT_scale=h_scales[:, tokens],
-                    rhs=up_piece[u][:, i, cols].bitcast(FP8X4),
-                    rhs_scale=up_planes[4 * j : P, r * KV + half * BANK : r * KV + (half + 1) * BANK],
-                    start=False,
-                    stop=(group == GROUPS - 1),
-                )
+                for i in range(UP_PIECE):
+                    group = u * UP_PIECE + i
+                    r, j = divmod(group, ROUND)
+                    tokens = slice(group * P, (group + 1) * P)
+                    nc.tensor.matmul_mx(
+                        out=kv_sum[half][:],
+                        lhsT=h_codes[:, tokens].bitcast(FP8X4),
+                        lhsT_scale=h_scales[:, tokens],
+                        rhs=up_piece[u][:, i, half * BANK : (half + 1) * BANK].bitcast(FP8X4),
+                        rhs_scale=up_planes[4 * j : P, r * KV + half * BANK : r * KV + (half + 1) * BANK],
+                        start=False,
+                        stop=(group == GROUPS - 1),
+                    )
 
-        for step in range(GROUPS + UP_LAG):
+        def adapter_step(step):
             if step < GROUPS:
                 multiply_down(step)
                 if step % ROUND == ROUND - 1:
@@ -291,8 +291,31 @@ def tile_attention_pa_k_kernel(
                     regroup((step - 1) // ROUND)
             if 0 <= step - 2 < GROUPS and (step - 2) % ROUND == ROUND - 1:
                 quantise((step - 2) // ROUND)
-            if step >= UP_LAG:
-                multiply_up(step - UP_LAG)
+
+        for step in range(UP_LAG):
+            adapter_step(step)
+
+        query_bank = banks.tile([P, BANK], F32, tag="product")
+        multiply_x(query_bank[:], qkv_words[:, 0:BANK], first_planes[0:P, 0:BANK], True, True)
+        query = keep.tile([P, BANK], F32)
+        nc.scalar.copy(out=query[:], in_=query_bank[:])
+        nc.scalar.dma_start(out=out[0][:, 0:BANK], in_=query[:])
+
+        kv_sum = [sums.tile([P, BANK], F32, name="kv_sum%d" % half) for half in range(KV // BANK)]
+        for half in range(KV // BANK):
+            block = 1 + half
+            multiply_x(
+                kv_sum[half][:],
+                qkv_words[:, block * BANK : (block + 1) * BANK],
+                first_planes[4 * block : P, 0:BANK],
+                True,
+                False,
+            )
+
+        for u in range(UP_PIECES):
+            for step in range(UP_LAG + u * UP_PIECE, UP_LAG + (u + 1) * UP_PIECE):
+                adapter_step(step)
+            multiply_up(u)
 
         kv_out = keep.tile([P, KV], F32)
         for half in range(KV // BANK):

@@ -23,13 +23,16 @@ ADAPTERS = 2
 QUADRANTS = 4
 
 GROUPS = ADAPTERS * HIDDEN // K_PASS
+PAIR = 2
+PAIRS = GROUPS // PAIR
 ROUND = 4
 ROUNDS = GROUPS // ROUND
-UP_PIECE = 2
-UP_PIECES = GROUPS // UP_PIECE
+ROUNDS_EACH = ROUNDS // ADAPTERS
+ROUND_PAIRS = ROUND // PAIR
+UP_LAG = 5
+DOWN_LEAD = 3
+LOAD_AHEAD = 2
 PIECE_BUFS = 16
-UP_LAG = 22
-RIDERS = 2
 
 FLOPS = 2 * P * (DIM * (DIM + KV) + ADAPTERS * (DIM * HIDDEN + HIDDEN * KV))
 
@@ -77,102 +80,101 @@ def tile_attention_pa_k_kernel(
 
         identity = keep.tile([P, P], F32)
         make_identity(nc, identity[:])
-        ones = keep.tile([P, P], BF16)
-        nc.gpsimd.memset(ones[:], 1.0)
         down_bias_rows = keep.tile([P, K_PASS], BF16)
         nc.gpsimd.memset(down_bias_rows[:], 0.0)
         up_bias_rows = keep.tile([P, KV], BF16)
         nc.gpsimd.memset(up_bias_rows[:], 0.0)
-        spare = keep.tile([P, 1], F32)
-        nc.vector.memset(spare[:], 0.0)
-        nc.scalar.activation(out=spare[:], in_=spare[:], func=TANH)
+        ones = keep.tile([P, P], BF16)
+        nc.gpsimd.memset(ones[:], 1.0)
 
         x_rows = keep.tile([P, DIM], BF16)
         nc.scalar.dma_start(out=x_rows[:], in_=x[0])
         for a in range(ADAPTERS):
             first = a * GROUPS // ADAPTERS
-            nc.gpsimd.dma_start(
+            nc.scalar.dma_start(
                 out=down_bias_rows[first : first + GROUPS // ADAPTERS, :],
                 in_=down_bias[a].rearrange("(g c) -> g c", c=K_PASS),
             )
+        spare = keep.tile([P, 1], F32)
+        nc.scalar.activation(out=spare[:], in_=identity[:, 0:1], func=TANH)
+
+        def load_planes(queue, view, planes, cols, count, rows_of):
+            for quadrant in range(QUADRANTS):
+                queue.dma_start(
+                    out=planes[32 * quadrant : 32 * quadrant + 4 * count, cols].bitcast(view),
+                    in_=rows_of(slice(4 * quadrant, 4 * quadrant + 4)).bitcast(view),
+                )
+
         for a in range(ADAPTERS):
             nc.gpsimd.dma_start(out=up_bias_rows[a : a + 1, :], in_=up_bias[a].rearrange("(o n) -> o n", o=1))
 
-        def plane_dmas(planes, cols, count, rows_of):
-            return [
-                (
-                    planes[32 * quadrant : 32 * quadrant + 4 * count, cols].bitcast(I32),
-                    rows_of(slice(4 * quadrant, 4 * quadrant + 4)).bitcast(I32),
-                )
-                for quadrant in range(QUADRANTS)
-            ]
+        down_piece = []
+        up_piece = []
 
-        def down_plane_dmas(a):
-            return plane_dmas(
+        def load_down_planes(a):
+            load_planes(
+                nc.sync,
+                I32,
                 first_planes,
                 slice(BANK + a * round_cols, BANK + (a + 1) * round_cols),
                 ROUND,
                 lambda rows: down_scales[a][0][rows, :].rearrange("r (j n) -> j r n", n=round_cols),
             )
 
-        def up_plane_dmas(r):
-            a = r // (ROUNDS // ADAPTERS)
-            first = (r % (ROUNDS // ADAPTERS)) * ROUND
-            return plane_dmas(
+        def load_down_piece():
+            a, j = divmod(len(down_piece), ROUNDS_EACH)
+            piece = pieces.tile([P, round_cols], I32, tag="piece", align_bytes=64)
+            nc.sync.dma_start(
+                out=piece[:],
+                in_=down_words[a][0]
+                .rearrange("p n t -> p (n t)")[:, j * round_cols * PACK : (j + 1) * round_cols * PACK]
+                .bitcast(I32),
+            )
+            down_piece.append(piece)
+
+        def load_up_piece():
+            a, j = divmod(len(up_piece), PAIRS // ADAPTERS)
+            piece = pieces.tile([P, PAIR, KV], I32, tag="piece", align_bytes=64)
+            nc.sync.dma_start(
+                out=piece[:],
+                in_=up_words[a][j * PAIR : (j + 1) * PAIR].rearrange("g p n t -> p g (n t)").bitcast(I32),
+            )
+            up_piece.append(piece)
+
+        def load_round():
+            if len(down_piece) < ROUNDS:
+                load_down_piece()
+            r = len(up_piece) // ROUND_PAIRS
+            a, j = divmod(r, ROUNDS_EACH)
+            load_planes(
+                nc.sync,
+                I32,
                 up_planes,
                 slice(r * KV, (r + 1) * KV),
                 ROUND,
-                lambda rows: up_scales[a][first : first + ROUND, rows, :],
+                lambda rows: up_scales[a][j * ROUND : (j + 1) * ROUND, rows, :],
             )
+            load_up_piece()
+            load_up_piece()
 
-        for destination, source in down_plane_dmas(0):
-            nc.sync.dma_start(out=destination, in_=source)
-        riders = down_plane_dmas(1) + plane_dmas(
+        load_down_piece()
+        load_down_planes(0)
+        load_down_piece()
+        load_planes(
+            nc.sync,
+            I32,
             first_planes,
             slice(0, BANK),
             3,
             lambda rows: Wqkv_scales[0][rows, :].rearrange("r (j n) -> j r n", n=BANK),
         )
-        for r in range(ROUNDS):
-            riders.extend(up_plane_dmas(r))
-        words_loaded = []
-
-        def load_words(destination, source):
-            nc.sync.dma_start(out=destination, in_=source)
-            n = len(words_loaded)
-            for rider_destination, rider_source in riders[RIDERS * n : RIDERS * (n + 1)]:
-                nc.sync.dma_start(out=rider_destination, in_=rider_source)
-            words_loaded.append(destination)
-
-        down_piece = []
-        for r in range(ROUNDS):
-            a = r // (ROUNDS // ADAPTERS)
-            first = (r % (ROUNDS // ADAPTERS)) * round_cols * PACK
-            piece = pieces.tile([P, round_cols], I32, tag="piece", align_bytes=64)
-            load_words(
-                piece[:],
-                down_words[a][0].rearrange("p n t -> p (n t)")[:, first : first + round_cols * PACK].bitcast(I32),
-            )
-            down_piece.append(piece)
-
         qkv_words = keep.tile([P, DIM + KV], I32, align_bytes=64)
-        load_words(qkv_words[:], Wqkv_words[0].rearrange("p n t -> p (n t)").bitcast(I32))
-
-        up_piece = []
-
-        def load_up_piece():
-            u = len(up_piece)
-            a = u // (UP_PIECES // ADAPTERS)
-            first = (u % (UP_PIECES // ADAPTERS)) * UP_PIECE
-            piece = pieces.tile([P, UP_PIECE, KV], I32, tag="piece", align_bytes=64)
-            load_words(
-                piece[:],
-                up_words[a][first : first + UP_PIECE].rearrange("g p n t -> p g (n t)").bitcast(I32),
-            )
-            up_piece.append(piece)
-
-        for u in range(PIECE_BUFS - ROUNDS):
-            load_up_piece()
+        nc.sync.dma_start(out=qkv_words[:], in_=Wqkv_words[0].rearrange("p n t -> p (n t)").bitcast(I32))
+        load_down_piece()
+        load_down_planes(1)
+        assert len(down_piece) == DOWN_LEAD
+        for r in range(LOAD_AHEAD):
+            load_round()
 
         x_words = x_rows[:].bitcast(F32)
         x_turned = banks.tile([P, 2, P], F32, tag="turned")
@@ -195,13 +197,6 @@ def tile_attention_pa_k_kernel(
         down_bias_cols = keep.tile([P, PACK, GROUPS], F32)
         nc.vector.tensor_copy(out=down_bias_cols[:], in_=bias_turned[:, :, 0:GROUPS])
 
-        kv_bias = keep.tile([P, KV], F32)
-        for half in range(KV // BANK):
-            cols = slice(half * BANK, (half + 1) * BANK)
-            spread = banks.tile([P, BANK], F32, tag="product")
-            nc.tensor.matmul(out=spread[:], lhsT=ones[:], rhs=up_bias_rows[:, cols], start=True, stop=True)
-            nc.scalar.copy(out=kv_bias[:, cols], in_=spread[:])
-
         def multiply_x(bank, words, planes, start, stop):
             nc.tensor.matmul_mx(
                 out=bank,
@@ -215,41 +210,49 @@ def tile_attention_pa_k_kernel(
 
         h_codes = keep.tile([P, GROUPS * P], U32, align_bytes=64)
         h_scales = keep.tile([P, GROUPS * P], U8, align_bytes=64)
+        products = {}
         sorted_rows = {}
         h_planes = {}
         h_grouped = {}
 
-        def multiply_down(group):
-            r, c = divmod(group, ROUND)
-            a, j = divmod(r, ROUNDS // ADAPTERS)
-            first = BANK + a * round_cols + c * BANK
-            product = banks.tile([P, BANK], F32, tag="product")
-            multiply_x(
-                product[:],
-                down_piece[r][:, c * BANK : (c + 1) * BANK],
-                first_planes[4 * j : P, first : first + BANK],
-                True,
-                True,
-            )
-            by_t = sorted_pool.tile([P, PACK, P], F32, tag="by_t")
-            nc.vector.tensor_copy(out=by_t[:], in_=product[:].rearrange("w (p t) -> w t p", t=PACK))
-            sorted_rows[group] = by_t
+        def multiply_down(pair):
+            for group in range(pair * PAIR, (pair + 1) * PAIR):
+                r, c = divmod(group, ROUND)
+                a, j = divmod(r, ROUNDS_EACH)
+                first = BANK + a * round_cols + c * BANK
+                product = banks.tile([P, BANK], F32, tag="product")
+                multiply_x(
+                    product[:],
+                    down_piece[r][:, c * BANK : (c + 1) * BANK],
+                    first_planes[4 * j : P, first : first + BANK],
+                    True,
+                    True,
+                )
+                products[group] = product
+            for group in range(pair * PAIR, (pair + 1) * PAIR):
+                by_t = sorted_pool.tile([P, PACK, P], F32, tag="by_t")
+                nc.vector.tensor_copy(out=by_t[:], in_=products[group][:].rearrange("w (p t) -> w t p", t=PACK))
+                sorted_rows[group] = by_t
 
-        def turn_and_squash(group):
-            r, c = divmod(group, ROUND)
-            if c == 0:
+        def turn_and_squash(pair):
+            r = pair * PAIR // ROUND
+            if pair * PAIR % ROUND == 0:
                 planes = hidden_pool.tile([P, ROUND, PACK, P], BF16, tag="planes")
                 h_planes[r] = planes
-            turned = banks.tile([P, PACK, P], F32, tag="turned")
-            for t in range(PACK):
-                nc.tensor.transpose(turned[:, t, :], sorted_rows[group][:, t, :], identity[:])
-            for t in range(PACK):
-                nc.scalar.activation(
-                    out=h_planes[r][:, c, t, :],
-                    in_=turned[:, t, :],
-                    func=TANH,
-                    bias=down_bias_cols[:, t, group : group + 1],
-                )
+            turned_banks = {}
+            for group in range(pair * PAIR, (pair + 1) * PAIR):
+                turned = banks.tile([P, PACK, P], F32, tag="turned")
+                for t in range(PACK):
+                    nc.tensor.transpose(turned[:, t, :], sorted_rows[group][:, t, :], identity[:])
+                turned_banks[group] = turned
+            for group in range(pair * PAIR, (pair + 1) * PAIR):
+                for t in range(PACK):
+                    nc.scalar.activation(
+                        out=h_planes[r][:, group % ROUND, t, :],
+                        in_=turned_banks[group][:, t, :],
+                        func=TANH,
+                        bias=down_bias_cols[:, t, group : group + 1],
+                    )
 
         def regroup(r):
             grouped = hidden_pool.tile([P, ROUND, P, PACK], BF16, tag="grouped", align_bytes=64)
@@ -264,36 +267,43 @@ def tile_attention_pa_k_kernel(
                 in_=h_grouped[r][:].rearrange("p g w t -> p (g w t)"),
             )
 
-        def multiply_up(u):
+        def multiply_up(pair):
             for half in range(KV // BANK):
-                for i in range(UP_PIECE):
-                    group = u * UP_PIECE + i
+                for i in range(PAIR):
+                    group = pair * PAIR + i
                     r, j = divmod(group, ROUND)
                     tokens = slice(group * P, (group + 1) * P)
                     nc.tensor.matmul_mx(
                         out=kv_sum[half][:],
                         lhsT=h_codes[:, tokens].bitcast(FP8X4),
                         lhsT_scale=h_scales[:, tokens],
-                        rhs=up_piece[u][:, i, half * BANK : (half + 1) * BANK].bitcast(FP8X4),
+                        rhs=up_piece[pair][:, i, half * BANK : (half + 1) * BANK].bitcast(FP8X4),
                         rhs_scale=up_planes[4 * j : P, r * KV + half * BANK : r * KV + (half + 1) * BANK],
                         start=False,
                         stop=(group == GROUPS - 1),
                     )
 
-        def adapter_step(step):
-            if step < GROUPS:
+        def make_h(step):
+            if step < PAIRS:
                 multiply_down(step)
-                if step % ROUND == ROUND - 1:
-                    load_up_piece()
-            if 0 <= step - 1 < GROUPS:
+            if 0 <= step - 1 < PAIRS:
                 turn_and_squash(step - 1)
-                if (step - 1) % ROUND == ROUND - 1:
-                    regroup((step - 1) // ROUND)
-            if 0 <= step - 2 < GROUPS and (step - 2) % ROUND == ROUND - 1:
-                quantise((step - 2) // ROUND)
+            if 0 <= step - 2 < PAIRS and (step - 2) % ROUND_PAIRS == ROUND_PAIRS - 1:
+                regroup((step - 2) // ROUND_PAIRS)
+            if 0 <= step - 3 < PAIRS and (step - 3) % ROUND_PAIRS == ROUND_PAIRS - 1:
+                quantise((step - 3) // ROUND_PAIRS)
+            if step % ROUND_PAIRS == ROUND_PAIRS - 1 and len(up_piece) < PAIRS:
+                load_round()
 
         for step in range(UP_LAG):
-            adapter_step(step)
+            make_h(step)
+
+        kv_bias = keep.tile([P, KV], F32)
+        for half in range(KV // BANK):
+            cols = slice(half * BANK, (half + 1) * BANK)
+            spread = banks.tile([P, BANK], F32, tag="product")
+            nc.tensor.matmul(out=spread[:], lhsT=ones[:], rhs=up_bias_rows[:, cols], start=True, stop=True)
+            nc.scalar.copy(out=kv_bias[:, cols], in_=spread[:])
 
         query_bank = banks.tile([P, BANK], F32, tag="product")
         multiply_x(query_bank[:], qkv_words[:, 0:BANK], first_planes[0:P, 0:BANK], True, True)
@@ -312,10 +322,9 @@ def tile_attention_pa_k_kernel(
                 False,
             )
 
-        for u in range(UP_PIECES):
-            for step in range(UP_LAG + u * UP_PIECE, UP_LAG + (u + 1) * UP_PIECE):
-                adapter_step(step)
-            multiply_up(u)
+        for pair in range(PAIRS):
+            make_h(pair + UP_LAG)
+            multiply_up(pair)
 
         kv_out = keep.tile([P, KV], F32)
         for half in range(KV // BANK):

@@ -107,6 +107,16 @@ def tile_attention_pa_k_kernel(
 
         for a in range(ADAPTERS):
             nc.gpsimd.dma_start(out=up_bias_rows[a : a + 1, :], in_=up_bias[a].rearrange("(o n) -> o n", o=1))
+        for r in range(ROUNDS):
+            a, j = divmod(r, ROUNDS_EACH)
+            load_planes(
+                nc.gpsimd,
+                F32,
+                up_planes,
+                slice(r * KV, (r + 1) * KV),
+                ROUND,
+                lambda rows: up_scales[a][j * ROUND : (j + 1) * ROUND, rows, :],
+            )
 
         down_piece = []
         up_piece = []
@@ -144,16 +154,6 @@ def tile_attention_pa_k_kernel(
         def load_round():
             if len(down_piece) < ROUNDS:
                 load_down_piece()
-            r = len(up_piece) // ROUND_PAIRS
-            a, j = divmod(r, ROUNDS_EACH)
-            load_planes(
-                nc.sync,
-                I32,
-                up_planes,
-                slice(r * KV, (r + 1) * KV),
-                ROUND,
-                lambda rows: up_scales[a][j * ROUND : (j + 1) * ROUND, rows, :],
-            )
             load_up_piece()
             load_up_piece()
 

@@ -98,20 +98,34 @@ def tile_attention_pa_k_kernel(
         spare = keep.tile([P, 1], F32)
         nc.scalar.activation(out=spare[:], in_=identity[:, 0:1], func=TANH)
 
-        def load_planes(queue, view, planes, cols, count, rows_of):
+        def load_planes(planes, cols, count, rows_of):
             for quadrant in range(QUADRANTS):
-                queue.dma_start(
-                    out=planes[32 * quadrant : 32 * quadrant + 4 * count, cols].bitcast(view),
-                    in_=rows_of(slice(4 * quadrant, 4 * quadrant + 4)).bitcast(view),
+                nc.gpsimd.dma_start(
+                    out=planes[32 * quadrant : 32 * quadrant + 4 * count, cols].bitcast(F32),
+                    in_=rows_of(slice(4 * quadrant, 4 * quadrant + 4)).bitcast(F32),
                 )
 
+        def load_down_planes(a):
+            load_planes(
+                first_planes,
+                slice(BANK + a * round_cols, BANK + (a + 1) * round_cols),
+                ROUND,
+                lambda rows: down_scales[a][0][rows, :].rearrange("r (j n) -> j r n", n=round_cols),
+            )
+
+        load_down_planes(0)
+        load_planes(
+            first_planes,
+            slice(0, BANK),
+            3,
+            lambda rows: Wqkv_scales[0][rows, :].rearrange("r (j n) -> j r n", n=BANK),
+        )
+        load_down_planes(1)
         for a in range(ADAPTERS):
             nc.gpsimd.dma_start(out=up_bias_rows[a : a + 1, :], in_=up_bias[a].rearrange("(o n) -> o n", o=1))
         for r in range(ROUNDS):
             a, j = divmod(r, ROUNDS_EACH)
             load_planes(
-                nc.gpsimd,
-                F32,
                 up_planes,
                 slice(r * KV, (r + 1) * KV),
                 ROUND,
@@ -120,16 +134,6 @@ def tile_attention_pa_k_kernel(
 
         down_piece = []
         up_piece = []
-
-        def load_down_planes(a):
-            load_planes(
-                nc.sync,
-                I32,
-                first_planes,
-                slice(BANK + a * round_cols, BANK + (a + 1) * round_cols),
-                ROUND,
-                lambda rows: down_scales[a][0][rows, :].rearrange("r (j n) -> j r n", n=round_cols),
-            )
 
         def load_down_piece():
             a, j = divmod(len(down_piece), ROUNDS_EACH)
@@ -158,20 +162,10 @@ def tile_attention_pa_k_kernel(
             load_up_piece()
 
         load_down_piece()
-        load_down_planes(0)
         load_down_piece()
-        load_planes(
-            nc.sync,
-            I32,
-            first_planes,
-            slice(0, BANK),
-            3,
-            lambda rows: Wqkv_scales[0][rows, :].rearrange("r (j n) -> j r n", n=BANK),
-        )
         qkv_words = keep.tile([P, DIM + KV], I32, align_bytes=64)
         nc.sync.dma_start(out=qkv_words[:], in_=Wqkv_words[0].rearrange("p n t -> p (n t)").bitcast(I32))
         load_down_piece()
-        load_down_planes(1)
         assert len(down_piece) == DOWN_LEAD
         for r in range(LOAD_AHEAD):
             load_round()

@@ -30,9 +30,9 @@ ROUNDS = GROUPS // ROUND
 ROUNDS_EACH = ROUNDS // ADAPTERS
 ROUND_PAIRS = ROUND // PAIR
 UP_LAG = 5
-DOWN_LEAD = 3
-LOAD_AHEAD = 2
-PIECE_BUFS = 16
+DOWN_ROUNDS = 2
+DOWN_BUFS = 3
+UP_BUFS = 6
 
 FLOPS = 2 * P * (DIM * (DIM + KV) + ADAPTERS * (DIM * HIDDEN + HIDDEN * KV))
 
@@ -66,11 +66,14 @@ def tile_attention_pa_k_kernel(
 
     with ExitStack() as pools:
         keep = pools.enter_context(tc.tile_pool(name="keep", bufs=1))
-        pieces = pools.enter_context(tc.tile_pool(name="pieces", bufs=PIECE_BUFS))
+        down_pool = pools.enter_context(tc.tile_pool(name="down", bufs=DOWN_BUFS))
+        up_pool = pools.enter_context(tc.tile_pool(name="up", bufs=UP_BUFS))
+        code_pool = pools.enter_context(tc.tile_pool(name="codes", bufs=3))
         sorted_pool = pools.enter_context(tc.tile_pool(name="sorted", bufs=4))
         hidden_pool = pools.enter_context(tc.tile_pool(name="hidden", bufs=2))
         sums = pools.enter_context(tc.psum_pool(name="sums", bufs=1))
         banks = pools.enter_context(tc.psum_pool(name="banks", bufs=3))
+        pools.enter_context(tc.manual_schedule())
 
         round_cols = ROUND * BANK
         first_planes = keep.tile([P, BANK + ADAPTERS * round_cols], U8, align_bytes=64)
@@ -81,11 +84,11 @@ def tile_attention_pa_k_kernel(
         identity = keep.tile([P, P], F32)
         make_identity(nc, identity[:])
         down_bias_rows = keep.tile([P, K_PASS], BF16)
-        nc.gpsimd.memset(down_bias_rows[:], 0.0)
+        nc.vector.memset(down_bias_rows[:], 0.0)
         up_bias_rows = keep.tile([P, KV], BF16)
-        nc.gpsimd.memset(up_bias_rows[:], 0.0)
+        nc.vector.memset(up_bias_rows[:], 0.0)
         ones = keep.tile([P, P], BF16)
-        nc.gpsimd.memset(ones[:], 1.0)
+        nc.vector.memset(ones[:], 1.0)
 
         x_rows = keep.tile([P, DIM], BF16)
         nc.scalar.dma_start(out=x_rows[:], in_=x[0])
@@ -132,43 +135,56 @@ def tile_attention_pa_k_kernel(
                 lambda rows: up_scales[a][j * ROUND : (j + 1) * ROUND, rows, :],
             )
 
-        down_piece = []
-        up_piece = []
+        down_of = {}
+        up_of = {}
 
-        def load_down_piece():
-            a, j = divmod(len(down_piece), ROUNDS_EACH)
-            piece = pieces.tile([P, round_cols], I32, tag="piece", align_bytes=64)
+        def load_down(i):
+            first_round = i * DOWN_ROUNDS
+            a, j = divmod(first_round, ROUNDS_EACH)
+            width = DOWN_ROUNDS * round_cols
+            piece = down_pool.tile([P, width], I32, tag="piece", align_bytes=64)
+            first = j * round_cols
             nc.sync.dma_start(
                 out=piece[:],
                 in_=down_words[a][0]
-                .rearrange("p n t -> p (n t)")[:, j * round_cols * PACK : (j + 1) * round_cols * PACK]
+                .rearrange("p n t -> p (n t)")[:, first * PACK : (first + width) * PACK]
                 .bitcast(I32),
             )
-            down_piece.append(piece)
+            for i in range(DOWN_ROUNDS):
+                down_of[first_round + i] = piece[:, i * round_cols : (i + 1) * round_cols]
 
-        def load_up_piece():
-            a, j = divmod(len(up_piece), PAIRS // ADAPTERS)
-            piece = pieces.tile([P, PAIR, KV], I32, tag="piece", align_bytes=64)
+        def load_up(pool, tag, first_group, count, first_col, width):
+            a, g = divmod(first_group, GROUPS // ADAPTERS)
+            piece = pool.tile([P, count, width], I32, tag=tag, name=tag, align_bytes=64)
             nc.sync.dma_start(
                 out=piece[:],
-                in_=up_words[a][j * PAIR : (j + 1) * PAIR].rearrange("g p n t -> p g (n t)").bitcast(I32),
+                in_=up_words[a][g : g + count]
+                .rearrange("g p n t -> p g (n t)")[:, :, first_col * PACK : (first_col + width) * PACK]
+                .bitcast(I32),
             )
-            up_piece.append(piece)
+            for i in range(count):
+                for col in range(0, width, BANK):
+                    up_of[first_group + i, (first_col + col) // BANK] = piece[:, i, col : col + BANK]
 
-        def load_round():
-            if len(down_piece) < ROUNDS:
-                load_down_piece()
-            load_up_piece()
-            load_up_piece()
+        def load_up_round(r):
+            load_up(up_pool, "piece", r * ROUND, ROUND, 0, KV)
 
-        load_down_piece()
-        load_down_piece()
+        def load_last_round():
+            first = GROUPS - ROUND
+            load_up(keep, "last_pair", first, PAIR, 0, KV)
+            load_up(keep, "last_first_half", first + PAIR, PAIR, 0, BANK)
+            for i in range(PAIR):
+                load_up(keep, "last_second_half%d" % i, first + PAIR + i, 1, BANK, BANK)
+
+        load_down(0)
         qkv_words = keep.tile([P, DIM + KV], I32, align_bytes=64)
         nc.sync.dma_start(out=qkv_words[:], in_=Wqkv_words[0].rearrange("p n t -> p (n t)").bitcast(I32))
-        load_down_piece()
-        assert len(down_piece) == DOWN_LEAD
-        for r in range(LOAD_AHEAD):
-            load_round()
+        load_down(1)
+        load_up_round(0)
+        load_up_round(1)
+        load_down(2)
+        load_up_round(2)
+        load_up_round(3)
 
         x_words = x_rows[:].bitcast(F32)
         x_turned = banks.tile([P, 2, P], F32, tag="turned")
@@ -202,8 +218,8 @@ def tile_attention_pa_k_kernel(
                 stop=stop,
             )
 
-        h_codes = keep.tile([P, GROUPS * P], U32, align_bytes=64)
-        h_scales = keep.tile([P, GROUPS * P], U8, align_bytes=64)
+        h_codes = {}
+        h_scales = {}
         products = {}
         sorted_rows = {}
         h_planes = {}
@@ -217,7 +233,7 @@ def tile_attention_pa_k_kernel(
                 product = banks.tile([P, BANK], F32, tag="product")
                 multiply_x(
                     product[:],
-                    down_piece[r][:, c * BANK : (c + 1) * BANK],
+                    down_of[r][:, c * BANK : (c + 1) * BANK],
                     first_planes[4 * j : P, first : first + BANK],
                     True,
                     True,
@@ -254,24 +270,27 @@ def tile_attention_pa_k_kernel(
             h_grouped[r] = grouped
 
         def quantise(r):
-            cols = slice(r * ROUND * P, (r + 1) * ROUND * P)
+            codes = code_pool.tile([P, ROUND * P], U32, tag="codes", align_bytes=64)
+            scales = code_pool.tile([P, ROUND * P], U8, tag="scales", align_bytes=64)
             nc.vector.quantize_mx(
-                out=h_codes[:, cols].bitcast(FP8X4),
-                scales=h_scales[:, cols],
+                out=codes[:].bitcast(FP8X4),
+                scales=scales[:],
                 in_=h_grouped[r][:].rearrange("p g w t -> p (g w t)"),
             )
+            h_codes[r] = codes
+            h_scales[r] = scales
 
         def multiply_up(pair):
             for half in range(KV // BANK):
                 for i in range(PAIR):
                     group = pair * PAIR + i
                     r, j = divmod(group, ROUND)
-                    tokens = slice(group * P, (group + 1) * P)
+                    tokens = slice(j * P, (j + 1) * P)
                     nc.tensor.matmul_mx(
                         out=kv_sum[half][:],
-                        lhsT=h_codes[:, tokens].bitcast(FP8X4),
-                        lhsT_scale=h_scales[:, tokens],
-                        rhs=up_piece[pair][:, i, half * BANK : (half + 1) * BANK].bitcast(FP8X4),
+                        lhsT=h_codes[r][:, tokens].bitcast(FP8X4),
+                        lhsT_scale=h_scales[r][:, tokens],
+                        rhs=up_of[group, half].bitcast(FP8X4),
                         rhs_scale=up_planes[4 * j : P, r * KV + half * BANK : r * KV + (half + 1) * BANK],
                         start=False,
                         stop=(group == GROUPS - 1),
@@ -286,11 +305,11 @@ def tile_attention_pa_k_kernel(
                 regroup((step - 2) // ROUND_PAIRS)
             if 0 <= step - 3 < PAIRS and (step - 3) % ROUND_PAIRS == ROUND_PAIRS - 1:
                 quantise((step - 3) // ROUND_PAIRS)
-            if step % ROUND_PAIRS == ROUND_PAIRS - 1 and len(up_piece) < PAIRS:
-                load_round()
-
         for step in range(UP_LAG):
             make_h(step)
+        load_down(3)
+        load_up_round(4)
+        load_up_round(5)
 
         kv_bias = keep.tile([P, KV], F32)
         for half in range(KV // BANK):
@@ -303,7 +322,6 @@ def tile_attention_pa_k_kernel(
         multiply_x(query_bank[:], qkv_words[:, 0:BANK], first_planes[0:P, 0:BANK], True, True)
         query = keep.tile([P, BANK], F32)
         nc.scalar.copy(out=query[:], in_=query_bank[:])
-        nc.scalar.dma_start(out=out[0][:, 0:BANK], in_=query[:])
 
         kv_sum = [sums.tile([P, BANK], F32, name="kv_sum%d" % half) for half in range(KV // BANK)]
         for half in range(KV // BANK):
@@ -319,6 +337,10 @@ def tile_attention_pa_k_kernel(
         for pair in range(PAIRS):
             make_h(pair + UP_LAG)
             multiply_up(pair)
+            if pair == ROUND_PAIRS - 1:
+                load_up_round(6)
+                load_last_round()
+                nc.sync.dma_start(out=out[0][:, 0:BANK], in_=query[:])
 
         kv_out = keep.tile([P, KV], F32)
         for half in range(KV // BANK):

@@ -76,10 +76,11 @@ def tile_attention_pa_k_kernel(
         pools.enter_context(tc.manual_schedule())
 
         round_cols = ROUND * BANK
-        first_planes = keep.tile([P, BANK + ADAPTERS * round_cols], U8, align_bytes=64)
+        down_planes = keep.tile([P, ADAPTERS * round_cols], U8, align_bytes=64)
         up_planes = keep.tile([P, ROUNDS * KV], U8, align_bytes=64)
-        nc.vector.memset(first_planes[:].bitcast(I32), 0)
-        nc.vector.memset(up_planes[:].bitcast(I32), 0)
+        qkv_planes = keep.tile([P, DIM + KV], U8, align_bytes=64)
+        nc.vector.memset(down_planes[:].bitcast(I32), 0)
+        nc.vector.memset(qkv_planes[:].bitcast(I32), 0)
 
         identity = keep.tile([P, P], F32)
         make_identity(nc, identity[:])
@@ -89,6 +90,7 @@ def tile_attention_pa_k_kernel(
         nc.vector.memset(up_bias_rows[:], 0.0)
         ones = keep.tile([P, P], BF16)
         nc.vector.memset(ones[:], 1.0)
+        nc.vector.memset(up_planes[:].bitcast(I32), 0)
 
         x_rows = keep.tile([P, DIM], BF16)
         nc.scalar.dma_start(out=x_rows[:], in_=x[0])
@@ -98,6 +100,13 @@ def tile_attention_pa_k_kernel(
                 out=down_bias_rows[first : first + GROUPS // ADAPTERS, :],
                 in_=down_bias[a].rearrange("(g c) -> g c", c=K_PASS),
             )
+        for quadrant in range(QUADRANTS):
+            nc.scalar.dma_start(
+                out=qkv_planes[32 * quadrant : 32 * quadrant + 4, :].bitcast(F32),
+                in_=Wqkv_scales[0][4 * quadrant : 4 * quadrant + 4, :].bitcast(F32),
+            )
+        for a in range(ADAPTERS):
+            nc.scalar.dma_start(out=up_bias_rows[a : a + 1, :], in_=up_bias[a].rearrange("(o n) -> o n", o=1))
         spare = keep.tile([P, 1], F32)
         nc.scalar.activation(out=spare[:], in_=identity[:, 0:1], func=TANH)
 
@@ -110,23 +119,16 @@ def tile_attention_pa_k_kernel(
 
         def load_down_planes(a):
             load_planes(
-                first_planes,
-                slice(BANK + a * round_cols, BANK + (a + 1) * round_cols),
+                down_planes,
+                slice(a * round_cols, (a + 1) * round_cols),
                 ROUND,
                 lambda rows: down_scales[a][0][rows, :].rearrange("r (j n) -> j r n", n=round_cols),
             )
 
         load_down_planes(0)
-        load_planes(
-            first_planes,
-            slice(0, BANK),
-            3,
-            lambda rows: Wqkv_scales[0][rows, :].rearrange("r (j n) -> j r n", n=BANK),
-        )
-        load_down_planes(1)
-        for a in range(ADAPTERS):
-            nc.gpsimd.dma_start(out=up_bias_rows[a : a + 1, :], in_=up_bias[a].rearrange("(o n) -> o n", o=1))
         for r in range(ROUNDS):
+            if r == DOWN_ROUNDS:
+                load_down_planes(1)
             a, j = divmod(r, ROUNDS_EACH)
             load_planes(
                 up_planes,
@@ -229,12 +231,12 @@ def tile_attention_pa_k_kernel(
             for group in range(pair * PAIR, (pair + 1) * PAIR):
                 r, c = divmod(group, ROUND)
                 a, j = divmod(r, ROUNDS_EACH)
-                first = BANK + a * round_cols + c * BANK
+                first = a * round_cols + c * BANK
                 product = banks.tile([P, BANK], F32, tag="product")
                 multiply_x(
                     product[:],
                     down_of[r][:, c * BANK : (c + 1) * BANK],
-                    first_planes[4 * j : P, first : first + BANK],
+                    down_planes[4 * j : P, first : first + BANK],
                     True,
                     True,
                 )
@@ -319,7 +321,7 @@ def tile_attention_pa_k_kernel(
             nc.scalar.copy(out=kv_bias[:, cols], in_=spread[:])
 
         query_bank = banks.tile([P, BANK], F32, tag="product")
-        multiply_x(query_bank[:], qkv_words[:, 0:BANK], first_planes[0:P, 0:BANK], True, True)
+        multiply_x(query_bank[:], qkv_words[:, 0:BANK], qkv_planes[:, 0:BANK], True, True)
         query = keep.tile([P, BANK], F32)
         nc.scalar.copy(out=query[:], in_=query_bank[:])
 
@@ -329,7 +331,7 @@ def tile_attention_pa_k_kernel(
             multiply_x(
                 kv_sum[half][:],
                 qkv_words[:, block * BANK : (block + 1) * BANK],
-                first_planes[4 * block : P, 0:BANK],
+                qkv_planes[:, block * BANK : (block + 1) * BANK],
                 True,
                 False,
             )

@@ -158,13 +158,13 @@ def tile_attention_pa_k_kernel(
         def load_up(pool, tag, first_group, count, first_col, width):
             a, g = divmod(first_group, GROUPS // ADAPTERS)
             piece = pool.tile([P, count, width], I32, tag=tag, name=tag, align_bytes=64)
-            nc.sync.dma_start(
-                out=piece[:],
-                in_=up_words[a][g : g + count]
-                .rearrange("g p n t -> p g (n t)")[:, :, first_col * PACK : (first_col + width) * PACK]
-                .bitcast(I32),
-            )
             for i in range(count):
+                nc.sync.dma_start(
+                    out=piece[:, i],
+                    in_=up_words[a][g + i]
+                    .rearrange("p n t -> p (n t)")[:, first_col * PACK : (first_col + width) * PACK]
+                    .bitcast(I32),
+                )
                 for col in range(0, width, BANK):
                     up_of[first_group + i, (first_col + col) // BANK] = piece[:, i, col : col + BANK]
 

@@ -33,6 +33,7 @@ UP_LAG = 5
 DOWN_ROUNDS = 2
 DOWN_BUFS = 3
 UP_BUFS = 6
+LAST_COLS = BANK // 2
 
 FLOPS = 2 * P * (DIM * (DIM + KV) + ADAPTERS * (DIM * HIDDEN + HIDDEN * KV))
 
@@ -166,17 +167,17 @@ def tile_attention_pa_k_kernel(
                     .bitcast(I32),
                 )
                 for col in range(0, width, BANK):
-                    up_of[first_group + i, (first_col + col) // BANK] = piece[:, i, col : col + BANK]
+                    up_of[first_group + i, first_col + col] = piece[:, i, col : min(col + BANK, width)]
 
         def load_up_round(r):
             load_up(up_pool, "piece", r * ROUND, ROUND, 0, KV)
 
         def load_last_round():
             first = GROUPS - ROUND
-            load_up(keep, "last_pair", first, PAIR, 0, KV)
-            load_up(keep, "last_first_half", first + PAIR, PAIR, 0, BANK)
-            for i in range(PAIR):
-                load_up(keep, "last_second_half%d" % i, first + PAIR + i, 1, BANK, BANK)
+            load_up(keep, "last_full", first, PAIR, 0, KV)
+            load_up(keep, "last_half", first + PAIR, PAIR, 0, BANK)
+            for i in range(BANK // LAST_COLS):
+                load_up(keep, "last_cols%d" % i, first + PAIR, PAIR, BANK + i * LAST_COLS, LAST_COLS)
 
         load_down(0)
         qkv_words = keep.tile([P, DIM + KV], I32, align_bytes=64)
@@ -282,21 +283,21 @@ def tile_attention_pa_k_kernel(
             h_codes[r] = codes
             h_scales[r] = scales
 
-        def multiply_up(pair):
-            for half in range(KV // BANK):
-                for i in range(PAIR):
-                    group = pair * PAIR + i
-                    r, j = divmod(group, ROUND)
-                    tokens = slice(j * P, (j + 1) * P)
-                    nc.tensor.matmul_mx(
-                        out=kv_sum[half][:],
-                        lhsT=h_codes[r][:, tokens].bitcast(FP8X4),
-                        lhsT_scale=h_scales[r][:, tokens],
-                        rhs=up_of[group, half].bitcast(FP8X4),
-                        rhs_scale=up_planes[4 * j : P, r * KV + half * BANK : r * KV + (half + 1) * BANK],
-                        start=False,
-                        stop=(group == GROUPS - 1),
-                    )
+        def multiply_up(bank, pair, first_col, width, start, stop):
+            for i in range(PAIR):
+                group = pair * PAIR + i
+                r, j = divmod(group, ROUND)
+                tokens = slice(j * P, (j + 1) * P)
+                plane_cols = slice(r * KV + first_col, r * KV + first_col + width)
+                nc.tensor.matmul_mx(
+                    out=bank,
+                    lhsT=h_codes[r][:, tokens].bitcast(FP8X4),
+                    lhsT_scale=h_scales[r][:, tokens],
+                    rhs=up_of[group, first_col].bitcast(FP8X4),
+                    rhs_scale=up_planes[4 * j : P, plane_cols],
+                    start=start and i == 0,
+                    stop=stop and i == PAIR - 1,
+                )
 
         def make_h(step):
             if step < PAIRS:
@@ -336,16 +337,33 @@ def tile_attention_pa_k_kernel(
                 False,
             )
 
-        for pair in range(PAIRS):
+        kv_out = keep.tile([P, KV], F32)
+
+        def add(cols, bank, other):
+            nc.vector.tensor_tensor(out=kv_out[:, cols], in0=bank, in1=other[:, cols], op=ADD)
+
+        def store(cols):
+            nc.sync.dma_start(out=out[0][:, DIM + cols.start : DIM + cols.stop], in_=kv_out[:, cols])
+
+        first_half = slice(0, BANK)
+        second_half = slice(BANK, KV)
+        last = PAIRS - 1
+        for pair in range(last):
             make_h(pair + UP_LAG)
-            multiply_up(pair)
+            multiply_up(kv_sum[0][:], pair, 0, BANK, False, False)
+            multiply_up(kv_sum[1][:], pair, BANK, BANK, False, pair == last - 1)
             if pair == ROUND_PAIRS - 1:
                 load_up_round(6)
                 load_last_round()
                 nc.sync.dma_start(out=out[0][:, 0:BANK], in_=query[:])
 
-        kv_out = keep.tile([P, KV], F32)
-        for half in range(KV // BANK):
-            cols = slice(half * BANK, (half + 1) * BANK)
-            nc.vector.tensor_tensor(out=kv_out[:, cols], in0=kv_sum[half][:], in1=kv_bias[:, cols], op=ADD)
-            nc.sync.dma_start(out=out[0][:, BANK + half * BANK : BANK + (half + 1) * BANK], in_=kv_out[:, cols])
+        add(second_half, kv_sum[1][:], kv_bias)
+        multiply_up(kv_sum[0][:], last, 0, BANK, False, True)
+        add(first_half, kv_sum[0][:], kv_bias)
+        store(first_half)
+        for first_col in range(BANK, KV, LAST_COLS):
+            cols = slice(first_col, first_col + LAST_COLS)
+            bank = banks.tile([P, LAST_COLS], F32, tag="product")
+            multiply_up(bank[:], last, first_col, LAST_COLS, True, True)
+            add(cols, bank[:], kv_out)
+            store(cols)

from contextlib import ExitStack

import concourse.mybir as mybir
from concourse.masks import make_identity

F32 = mybir.dt.float32
BF16 = mybir.dt.bfloat16
I32 = mybir.dt.int32
U32 = mybir.dt.uint32
U8 = mybir.dt.uint8
FP8X4 = mybir.dt.float8_e4m3fn_x4
TANH = mybir.ActivationFunctionType.Tanh
ADD = mybir.AluOpType.add

P = 128
PACK = 4
K_PASS = P * PACK
BANK = 512
DIM = 512
HIDDEN = 8192
KV = 1024
ADAPTERS = 2
QUADRANTS = 4

GROUPS = ADAPTERS * HIDDEN // K_PASS
PAIR = 2
PAIRS = GROUPS // PAIR
ROUND = 4
ROUNDS = GROUPS // ROUND
ROUNDS_EACH = ROUNDS // ADAPTERS
ROUND_PAIRS = ROUND // PAIR
UP_LAG = 5
DOWN_ROUNDS = 2
DOWN_BUFS = 3
UP_BUFS = 6
LAST_COLS = BANK // 2

FLOPS = 2 * P * (DIM * (DIM + KV) + ADAPTERS * (DIM * HIDDEN + HIDDEN * KV))


def tile_attention_pa_k_kernel(
    tc,
    x,
    Wqkv_words,
    Wqkv_scales,
    down_w_words,
    down_w_scales,
    down_b,
    up_w_words,
    up_w_scales,
    up_b,
    pdown_w_words,
    pdown_w_scales,
    pdown_b,
    pup_w_words,
    pup_w_scales,
    pup_b,
    out,
):
    nc = tc.nc
    down_words = [pdown_w_words, down_w_words]
    down_scales = [pdown_w_scales, down_w_scales]
    down_bias = [pdown_b, down_b]
    up_words = [pup_w_words, up_w_words]
    up_scales = [pup_w_scales, up_w_scales]
    up_bias = [pup_b, up_b]

    with ExitStack() as pools:
        keep = pools.enter_context(tc.tile_pool(name="keep", bufs=1))
        down_pool = pools.enter_context(tc.tile_pool(name="down", bufs=DOWN_BUFS))
        up_pool = pools.enter_context(tc.tile_pool(name="up", bufs=UP_BUFS))
        code_pool = pools.enter_context(tc.tile_pool(name="codes", bufs=3))
        sorted_pool = pools.enter_context(tc.tile_pool(name="sorted", bufs=4))
        hidden_pool = pools.enter_context(tc.tile_pool(name="hidden", bufs=2))
        sums = pools.enter_context(tc.psum_pool(name="sums", bufs=1))
        banks = pools.enter_context(tc.psum_pool(name="banks", bufs=3))
        pools.enter_context(tc.manual_schedule())

        round_cols = ROUND * BANK
        down_planes = keep.tile([P, ADAPTERS * round_cols], U8, align_bytes=64)
        up_planes = keep.tile([P, ROUNDS * KV], U8, align_bytes=64)
        qkv_planes = keep.tile([P, DIM + KV], U8, align_bytes=64)
        nc.vector.memset(down_planes[:].bitcast(I32), 0)
        nc.vector.memset(qkv_planes[:].bitcast(I32), 0)

        identity = keep.tile([P, P], F32)
        make_identity(nc, identity[:])
        down_bias_rows = keep.tile([P, K_PASS], BF16)
        nc.vector.memset(down_bias_rows[:], 0.0)
        up_bias_rows = keep.tile([P, KV], BF16)
        nc.vector.memset(up_bias_rows[:], 0.0)
        ones = keep.tile([P, P], BF16)
        nc.vector.memset(ones[:], 1.0)
        nc.vector.memset(up_planes[:].bitcast(I32), 0)

        x_rows = keep.tile([P, DIM], BF16)
        nc.scalar.dma_start(out=x_rows[:], in_=x[0])
        for a in range(ADAPTERS):
            first = a * GROUPS // ADAPTERS
            nc.scalar.dma_start(
                out=down_bias_rows[first : first + GROUPS // ADAPTERS, :],
                in_=down_bias[a].rearrange("(g c) -> g c", c=K_PASS),
            )
        for quadrant in range(QUADRANTS):
            nc.scalar.dma_start(
                out=qkv_planes[32 * quadrant : 32 * quadrant + 4, :].bitcast(F32),
                in_=Wqkv_scales[0][4 * quadrant : 4 * quadrant + 4, :].bitcast(F32),
            )
        for a in range(ADAPTERS):
            nc.scalar.dma_start(out=up_bias_rows[a : a + 1, :], in_=up_bias[a].rearrange("(o n) -> o n", o=1))
        spare = keep.tile([P, 1], F32)
        nc.scalar.activation(out=spare[:], in_=identity[:, 0:1], func=TANH)

        def load_planes(planes, cols, count, rows_of):
            for quadrant in range(QUADRANTS):
                nc.gpsimd.dma_start(
                    out=planes[32 * quadrant : 32 * quadrant + 4 * count, cols].bitcast(F32),
                    in_=rows_of(slice(4 * quadrant, 4 * quadrant + 4)).bitcast(F32),
                )

        def load_down_planes(a):
            load_planes(
                down_planes,
                slice(a * round_cols, (a + 1) * round_cols),
                ROUND,
                lambda rows: down_scales[a][0][rows, :].rearrange("r (j n) -> j r n", n=round_cols),
            )

        load_down_planes(0)
        for r in range(ROUNDS):
            if r == DOWN_ROUNDS:
                load_down_planes(1)
            a, j = divmod(r, ROUNDS_EACH)
            load_planes(
                up_planes,
                slice(r * KV, (r + 1) * KV),
                ROUND,
                lambda rows: up_scales[a][j * ROUND : (j + 1) * ROUND, rows, :],
            )

        down_of = {}
        up_of = {}

        def load_down(i):
            first_round = i * DOWN_ROUNDS
            a, j = divmod(first_round, ROUNDS_EACH)
            width = DOWN_ROUNDS * round_cols
            piece = down_pool.tile([P, width], I32, tag="piece", align_bytes=64)
            first = j * round_cols
            nc.sync.dma_start(
                out=piece[:],
                in_=down_words[a][0]
                .rearrange("p n t -> p (n t)")[:, first * PACK : (first + width) * PACK]
                .bitcast(I32),
            )
            for i in range(DOWN_ROUNDS):
                down_of[first_round + i] = piece[:, i * round_cols : (i + 1) * round_cols]

        def load_up(pool, tag, first_group, count, first_col, width):
            a, g = divmod(first_group, GROUPS // ADAPTERS)
            piece = pool.tile([P, count, width], I32, tag=tag, name=tag, align_bytes=64)
            for i in range(count):
                nc.sync.dma_start(
                    out=piece[:, i],
                    in_=up_words[a][g + i]
                    .rearrange("p n t -> p (n t)")[:, first_col * PACK : (first_col + width) * PACK]
                    .bitcast(I32),
                )
                for col in range(0, width, BANK):
                    up_of[first_group + i, first_col + col] = piece[:, i, col : min(col + BANK, width)]

        def load_up_round(r):
            load_up(up_pool, "piece", r * ROUND, ROUND, 0, KV)

        def load_last_round():
            first = GROUPS - ROUND
            load_up(keep, "last_full", first, PAIR, 0, KV)
            load_up(keep, "last_half", first + PAIR, PAIR, 0, BANK)
            for i in range(BANK // LAST_COLS):
                load_up(keep, "last_cols%d" % i, first + PAIR, PAIR, BANK + i * LAST_COLS, LAST_COLS)

        load_down(0)
        qkv_words = keep.tile([P, DIM + KV], I32, align_bytes=64)
        nc.sync.dma_start(out=qkv_words[:], in_=Wqkv_words[0].rearrange("p n t -> p (n t)").bitcast(I32))
        load_down(1)
        load_up_round(0)
        load_up_round(1)
        load_down(2)
        load_up_round(2)
        load_up_round(3)

        x_words = x_rows[:].bitcast(F32)
        x_turned = banks.tile([P, 2, P], F32, tag="turned")
        for u in range(2):
            nc.tensor.transpose(x_turned[:, u, :], x_words[:, u : DIM // 2 : 2], identity[:])
        x_grouped = keep.tile([P, K_PASS], BF16, align_bytes=64)
        nc.vector.tensor_copy(
            out=x_grouped[:].bitcast(F32).rearrange("p (w u) -> p w u", u=2),
            in_=x_turned[:].rearrange("p u w -> p w u"),
        )
        x_codes = keep.tile([P, P], U32, align_bytes=64)
        x_scales = keep.tile([P, P], U8, align_bytes=64)
        nc.vector.quantize_mx(out=x_codes[:].bitcast(FP8X4), scales=x_scales[:], in_=x_grouped[:])

        down_bias_sorted = keep.tile([P, PACK, P], F32)
        nc.vector.tensor_copy(out=down_bias_sorted[:], in_=down_bias_rows[:].rearrange("g (p t) -> g t p", t=PACK))
        bias_turned = banks.tile([P, PACK, P], F32, tag="turned")
        for t in range(PACK):
            nc.tensor.transpose(bias_turned[:, t, :], down_bias_sorted[:, t, :], identity[:])
        down_bias_cols = keep.tile([P, PACK, GROUPS], F32)
        nc.vector.tensor_copy(out=down_bias_cols[:], in_=bias_turned[:, :, 0:GROUPS])

        def multiply_x(bank, words, planes, start, stop):
            nc.tensor.matmul_mx(
                out=bank,
                lhsT=x_codes[:].bitcast(FP8X4),
                lhsT_scale=x_scales[:],
                rhs=words.bitcast(FP8X4),
                rhs_scale=planes,
                start=start,
                stop=stop,
            )

        h_codes = {}
        h_scales = {}
        products = {}
        sorted_rows = {}
        h_planes = {}
        h_grouped = {}

        def multiply_down(pair):
            for group in range(pair * PAIR, (pair + 1) * PAIR):
                r, c = divmod(group, ROUND)
                a, j = divmod(r, ROUNDS_EACH)
                first = a * round_cols + c * BANK
                product = banks.tile([P, BANK], F32, tag="product")
                multiply_x(
                    product[:],
                    down_of[r][:, c * BANK : (c + 1) * BANK],
                    down_planes[4 * j : P, first : first + BANK],
                    True,
                    True,
                )
                products[group] = product
            for group in range(pair * PAIR, (pair + 1) * PAIR):
                by_t = sorted_pool.tile([P, PACK, P], F32, tag="by_t")
                nc.vector.tensor_copy(out=by_t[:], in_=products[group][:].rearrange("w (p t) -> w t p", t=PACK))
                sorted_rows[group] = by_t

        def turn_and_squash(pair):
            r = pair * PAIR // ROUND
            if pair * PAIR % ROUND == 0:
                planes = hidden_pool.tile([P, ROUND, PACK, P], BF16, tag="planes")
                h_planes[r] = planes
            turned_banks = {}
            for group in range(pair * PAIR, (pair + 1) * PAIR):
                turned = banks.tile([P, PACK, P], F32, tag="turned")
                for t in range(PACK):
                    nc.tensor.transpose(turned[:, t, :], sorted_rows[group][:, t, :], identity[:])
                turned_banks[group] = turned
            for group in range(pair * PAIR, (pair + 1) * PAIR):
                for t in range(PACK):
                    nc.scalar.activation(
                        out=h_planes[r][:, group % ROUND, t, :],
                        in_=turned_banks[group][:, t, :],
                        func=TANH,
                        bias=down_bias_cols[:, t, group : group + 1],
                    )

        def regroup(r):
            grouped = hidden_pool.tile([P, ROUND, P, PACK], BF16, tag="grouped", align_bytes=64)
            nc.vector.tensor_copy(out=grouped[:], in_=h_planes[r][:].rearrange("p g t w -> p g w t"))
            h_grouped[r] = grouped

        def quantise(r):
            codes = code_pool.tile([P, ROUND * P], U32, tag="codes", align_bytes=64)
            scales = code_pool.tile([P, ROUND * P], U8, tag="scales", align_bytes=64)
            nc.vector.quantize_mx(
                out=codes[:].bitcast(FP8X4),
                scales=scales[:],
                in_=h_grouped[r][:].rearrange("p g w t -> p (g w t)"),
            )
            h_codes[r] = codes
            h_scales[r] = scales

        def multiply_up(bank, pair, first_col, width, start, stop):
            for i in range(PAIR):
                group = pair * PAIR + i
                r, j = divmod(group, ROUND)
                tokens = slice(j * P, (j + 1) * P)
                plane_cols = slice(r * KV + first_col, r * KV + first_col + width)
                nc.tensor.matmul_mx(
                    out=bank,
                    lhsT=h_codes[r][:, tokens].bitcast(FP8X4),
                    lhsT_scale=h_scales[r][:, tokens],
                    rhs=up_of[group, first_col].bitcast(FP8X4),
                    rhs_scale=up_planes[4 * j : P, plane_cols],
                    start=start and i == 0,
                    stop=stop and i == PAIR - 1,
                )

        def make_h(step):
            if step < PAIRS:
                multiply_down(step)
            if 0 <= step - 1 < PAIRS:
                turn_and_squash(step - 1)
            if 0 <= step - 2 < PAIRS and (step - 2) % ROUND_PAIRS == ROUND_PAIRS - 1:
                regroup((step - 2) // ROUND_PAIRS)
            if 0 <= step - 3 < PAIRS and (step - 3) % ROUND_PAIRS == ROUND_PAIRS - 1:
                quantise((step - 3) // ROUND_PAIRS)
        for step in range(UP_LAG):
            make_h(step)
        load_down(3)
        load_up_round(4)
        load_up_round(5)

        kv_bias = keep.tile([P, KV], F32)
        for half in range(KV // BANK):
            cols = slice(half * BANK, (half + 1) * BANK)
            spread = banks.tile([P, BANK], F32, tag="product")
            nc.tensor.matmul(out=spread[:], lhsT=ones[:], rhs=up_bias_rows[:, cols], start=True, stop=True)
            nc.scalar.copy(out=kv_bias[:, cols], in_=spread[:])

        query_bank = banks.tile([P, BANK], F32, tag="product")
        multiply_x(query_bank[:], qkv_words[:, 0:BANK], qkv_planes[:, 0:BANK], True, True)
        query = keep.tile([P, BANK], F32)
        nc.scalar.copy(out=query[:], in_=query_bank[:])

        kv_sum = [sums.tile([P, BANK], F32, name="kv_sum%d" % half) for half in range(KV // BANK)]
        for half in range(KV // BANK):
            block = 1 + half
            multiply_x(
                kv_sum[half][:],
                qkv_words[:, block * BANK : (block + 1) * BANK],
                qkv_planes[:, block * BANK : (block + 1) * BANK],
                True,
                False,
            )

        kv_out = keep.tile([P, KV], F32)

        def add(cols, bank, other):
            nc.vector.tensor_tensor(out=kv_out[:, cols], in0=bank, in1=other[:, cols], op=ADD)

        def store(cols):
            nc.sync.dma_start(out=out[0][:, DIM + cols.start : DIM + cols.stop], in_=kv_out[:, cols])

        first_half = slice(0, BANK)
        second_half = slice(BANK, KV)
        last = PAIRS - 1
        for pair in range(last):
            make_h(pair + UP_LAG)
            multiply_up(kv_sum[0][:], pair, 0, BANK, False, False)
            multiply_up(kv_sum[1][:], pair, BANK, BANK, False, pair == last - 1)
            if pair == ROUND_PAIRS - 1:
                load_up_round(6)
                load_last_round()
                nc.sync.dma_start(out=out[0][:, 0:BANK], in_=query[:])

        add(second_half, kv_sum[1][:], kv_bias)
        multiply_up(kv_sum[0][:], last, 0, BANK, False, True)
        add(first_half, kv_sum[0][:], kv_bias)
        store(first_half)
        for first_col in range(BANK, KV, LAST_COLS):
            cols = slice(first_col, first_col + LAST_COLS)
            bank = banks.tile([P, LAST_COLS], F32, tag="product")
            multiply_up(bank[:], last, first_col, LAST_COLS, True, True)
            add(cols, bank[:], kv_out)
            store(cols)
